import numpy as np
import ml_dtypes


def mxq(x, axis, fmt="e4m3"):
    dtype, down = {"e4m3": (ml_dtypes.float8_e4m3fn, 7), "e5m2": (ml_dtypes.float8_e5m2, 14)}[fmt]
    v = np.moveaxis(np.asarray(x, np.float32).astype(ml_dtypes.bfloat16).astype(np.float64), axis, -1)
    blocks = v.reshape(v.shape[:-1] + (-1, 32))
    amax = np.abs(blocks).max(-1, keepdims=True)
    byte = np.maximum(np.where(amax > 0, np.frexp(amax)[1] - 1 + 127, 0) - down, 1)
    scale = np.exp2(byte - 127.0)
    codes = (blocks / scale).astype(np.float32).astype(dtype).astype(np.float64)
    return np.moveaxis((codes * scale).reshape(v.shape), -1, axis)


WIDE = False


def mx_kscale(k):
    if not WIDE:
        return np.ones(k)
    levels = np.array([10, -10, 5, -5, 0])
    a = np.random.permutation(np.resize(levels, k // 512 * 4)).reshape(k // 512, 4)
    idx = np.arange(k)
    return np.exp2(a[idx // 512, idx % 128 // 32])


BF16 = ml_dtypes.bfloat16


def bf(x):
    return np.asarray(x, np.float32).astype(BF16)


def f64(x):
    return np.asarray(x).astype(np.float64)


B, SI, ST, DM, H, D = 1, 768, 256, 1024, 8, 128
S = ST + SI
HD = H * D
EPS = 1e-6


def rms_norm(x, gamma):
    var = np.mean(x * x, axis=-1, keepdims=True)
    return x * (1.0 / np.sqrt(var + EPS)) * gamma


def apply_rotary(x, cos, sin):
    xr = x.reshape(B, S, H, D // 2, 2)
    x1, x2 = xr[..., 0], xr[..., 1]
    rot = np.stack([-x2, x1], axis=-1).reshape(B, S, H, D)
    return x * cos[None, :, None, :] + rot * sin[None, :, None, :]


def heads(y):
    return y.reshape(B, -1, H, D)


def setup_inputs():
    s = mx_kscale(DM)
    w = 1.0 / np.sqrt(DM)
    pos = np.arange(S)[:, None]
    inv = 1.0 / (10000.0 ** (np.arange(0, D, 2) / D))
    ang = np.repeat(pos * inv[None, :], 2, axis=-1)
    inp = {"hidden_states": bf(np.random.standard_normal((B, SI, DM)) * s),
           "encoder_hidden_states": bf(np.random.standard_normal((B, ST, DM)) * s),
           "rope_cos": bf(np.cos(ang)), "rope_sin": bf(np.sin(ang))}
    for n in ["Wq", "Wk", "Waq", "Wak"]:
        inp[n] = bf(np.random.standard_normal((DM, HD)) * w / s[:, None])
    for n in ["bq", "bk", "baq", "bak"]:
        inp[n] = bf(np.random.standard_normal(HD) * 0.3)
    for n in ["g_q", "g_k", "g_aq", "g_ak"]:
        inp[n] = bf(1.5 * (1.0 + 0.1 * np.random.standard_normal(D)))
    return inp


def reference(hidden_states, encoder_hidden_states, rope_cos, rope_sin, Wq, bq, Wk, bk, Waq, baq, Wak, bak, g_q, g_k, g_aq, g_ak):
    xq = mxq(f64(hidden_states), 2, "e4m3")
    cq = mxq(f64(encoder_hidden_states), 2, "e4m3")
    q = rms_norm(heads((xq @ mxq(f64(Wq), 0, "e4m3")) + f64(bq)), f64(g_q))
    k = rms_norm(heads((xq @ mxq(f64(Wk), 0, "e4m3")) + f64(bk)), f64(g_k))
    eq = rms_norm(heads((cq @ mxq(f64(Waq), 0, "e4m3")) + f64(baq)), f64(g_aq))
    ek = rms_norm(heads((cq @ mxq(f64(Wak), 0, "e4m3")) + f64(bak)), f64(g_ak))
    q = np.concatenate([eq, q], axis=1)
    k = np.concatenate([ek, k], axis=1)
    return apply_rotary(q, f64(rope_cos), f64(rope_sin)), apply_rotary(k, f64(rope_cos), f64(rope_sin))

@@ -1,0 +1,277 @@
+from contextlib import ExitStack
+
+import concourse.mybir as mybir
+from concourse.masks import make_identity
+
+F32 = mybir.dt.float32
+BF16 = mybir.dt.bfloat16
+U32 = mybir.dt.uint32
+U8 = mybir.dt.uint8
+FP8X4 = mybir.dt.float8_e4m3fn_x4
+ALU = mybir.AluOpType
+ACT = mybir.ActivationFunctionType
+
+P = 128
+PACK = 4
+K_PASS = P * PACK
+DM = 1024
+PASSES = DM // K_PASS
+H = 8
+D = 128
+PAIRS = D // 2
+HD = H * D
+BANK = 512
+BANK_HEADS = BANK // D
+EPS = 1e-6
+
+TEXT_TILES = 2
+IMAGE_TILES = 6
+TOKEN_TILES = TEXT_TILES + IMAGE_TILES
+TEXT_ROWS = TEXT_TILES * P
+
+IMAGE_VECTOR_COLS = 640
+
+FLOPS = 2 * (TOKEN_TILES * P) * DM * (2 * HD)
+
+
+def tile_fluxjointattention_pa_kernel(
+    tc,
+    hidden_states,
+    encoder_hidden_states,
+    rope_cos,
+    rope_sin,
+    Wq,
+    Wk,
+    Waq,
+    Wak,
+    bq,
+    bk,
+    baq,
+    bak,
+    g_q,
+    g_k,
+    g_aq,
+    g_ak,
+    out_0,
+    out_1,
+):
+    nc = tc.nc
+    weights = (Wq, Wk, Waq, Wak)
+    biases = (bq, bk, baq, bak)
+    gains = (g_q, g_k, g_aq, g_ak)
+    outs = (out_0, out_1)
+
+    def token_rows(dram_rows, tile_lo, tiles):
+        rows = dram_rows[tile_lo * P : (tile_lo + tiles) * P, :]
+        return rows.rearrange("(p n) c -> p n c", n=tiles)
+
+    with ExitStack() as ctx:
+        keep = ctx.enter_context(tc.tile_pool(name="keep", bufs=1))
+        raw_pool = ctx.enter_context(tc.tile_pool(name="raw", bufs=2))
+        stage = ctx.enter_context(tc.tile_pool(name="stage", bufs=2))
+        work = ctx.enter_context(tc.tile_pool(name="work", bufs=3))
+        psum_t = ctx.enter_context(tc.psum_pool(name="psum_t", bufs=2))
+        psum_y = ctx.enter_context(tc.psum_pool(name="psum_y", bufs=6))
+
+        act_sb = keep.tile([P, TOKEN_TILES, DM], BF16)
+        nc.sync.dma_start(
+            out=act_sb[:, TEXT_TILES:, :],
+            in_=hidden_states.rearrange("b (p n) k -> p (b n) k", n=IMAGE_TILES),
+        )
+
+        def load_weight(m):
+            raw = raw_pool.tile([P, PASSES, PACK, HD], BF16, name="raw")
+            for g in range(PASSES):
+                nc.sync.dma_start(
+                    out=raw[:, g, :, :].rearrange("p (u e) n -> p u (e n)", e=2),
+                    in_=weights[m][g * K_PASS : (g + 1) * K_PASS, :].rearrange(
+                        "(u q e) n -> q u (e n)", u=2, e=2
+                    ),
+                )
+            return raw
+
+        raw_q = load_weight(0)
+        raw_k = load_weight(1)
+        nc.sync.dma_start(
+            out=act_sb[:, :TEXT_TILES, :],
+            in_=encoder_hidden_states.rearrange("b (p n) k -> p (b n) k", n=TEXT_TILES),
+        )
+
+        cos_sb = keep.tile([P, TOKEN_TILES, D], BF16)
+        sin_sb = keep.tile([P, TOKEN_TILES, D], BF16)
+        gain_bc = keep.tile([P, 4, D], BF16)
+        bias_bc = keep.tile([P, 4, HD], BF16)
+        for table_sb, table in ((cos_sb, rope_cos), (sin_sb, rope_sin)):
+            nc.scalar.dma_start(
+                out=table_sb[:, TEXT_TILES:, :], in_=token_rows(table, TEXT_TILES, IMAGE_TILES)
+            )
+            nc.scalar.dma_start(out=table_sb[:, :TEXT_TILES, :], in_=token_rows(table, 0, TEXT_TILES))
+        for m in range(4):
+            nc.scalar.dma_start(out=gain_bc[:, m, :], in_=gains[m].partition_broadcast(P))
+        for m in range(4):
+            nc.gpsimd.dma_start(out=bias_bc[:, m, :], in_=biases[m].partition_broadcast(P))
+
+        ident = keep.tile([P, P], F32)
+        make_identity(nc, ident[:])
+        eps_col = keep.tile([P, 1], F32)
+        nc.vector.memset(eps_col[:], EPS)
+
+        gain_pairs = gain_bc[:].rearrange("p m (i t) -> p m i t", t=2)
+        gain_other = keep.tile([P, 4, 2, PAIRS], BF16)
+        nc.vector.tensor_scalar_mul(out=gain_other[:, :, 0, :], in0=gain_pairs[:, :, :, 1], scalar1=-1.0)
+        nc.vector.tensor_copy(out=gain_other[:, :, 1, :], in_=gain_pairs[:, :, :, 0])
+
+        SAME, OTHER = 0, 1
+        rot = keep.tile([P, TOKEN_TILES, 2, 2, D], F32)
+        for stream, (tile_lo, tiles) in enumerate(((TEXT_TILES, IMAGE_TILES), (0, TEXT_TILES))):
+            tile_range = slice(tile_lo, tile_lo + tiles)
+            shape = [P, tiles, 2, PAIRS]
+            for qk in range(2):
+                m = 2 * stream + qk
+                nc.vector.tensor_tensor(
+                    out=rot[:, tile_range, qk, SAME, :].rearrange("p n (t i) -> p n t i", t=2),
+                    in0=cos_sb[:, tile_range, :].rearrange("p n (i t) -> p n t i", t=2),
+                    in1=gain_bc[:, m, :].rearrange("p (i t) -> p t i", t=2).unsqueeze(1).to_broadcast(shape),
+                    op=ALU.mult,
+                )
+                nc.vector.tensor_tensor(
+                    out=rot[:, tile_range, qk, OTHER, :].rearrange("p n (t i) -> p n t i", t=2),
+                    in0=sin_sb[:, tile_range, :].rearrange("p n (i t) -> p n t i", t=2),
+                    in1=gain_other[:, m, :, :].unsqueeze(1).to_broadcast(shape),
+                    op=ALU.mult,
+                )
+
+        act_words = act_sb[:].bitcast(F32)
+        act_codes = keep.tile([P, PASSES, TOKEN_TILES * P], U32, align_bytes=64)
+        act_scales = keep.tile([P, PASSES, TOKEN_TILES * P], U8, align_bytes=64)
+
+        def quantise_activations(first_tile):
+            grouped = stage.tile([P, PASSES, 2 * P, PACK], BF16, name="act_grouped", align_bytes=64)
+            grouped_words = grouped[:].bitcast(F32)
+            for j in range(2):
+                turned = psum_t.tile([P, PASSES * 2, P], F32, name="turned")
+                for w in range(PASSES * 2):
+                    nc.tensor.transpose(
+                        out=turned[:, w, :],
+                        in_=act_words[:, first_tile + j, w * P : (w + 1) * P],
+                        identity=ident[:],
+                    )
+                nc.scalar.copy(
+                    out=grouped_words[:, :, j * P : (j + 1) * P, :],
+                    in_=turned[:].rearrange("p (g u) r -> p g r u", u=2),
+                )
+            cols = slice(first_tile * P, (first_tile + 2) * P)
+            for g in range(PASSES):
+                nc.vector.quantize_mx(
+                    out=act_codes[:, g, cols].bitcast(FP8X4),
+                    scales=act_scales[:, g, cols],
+                    in_=grouped[:, g, :, :].rearrange("p r j -> p (r j)"),
+                )
+
+        w_codes = keep.tile([P, 4, PASSES, HD], U32, align_bytes=64)
+        w_scales = keep.tile([P, 4, PASSES, HD], U8, align_bytes=64)
+
+        def quantise_weight_pass(raw, m, g, vector_cols):
+            grouped = stage.tile([P, HD, PACK], BF16, name="w_grouped", align_bytes=64)
+            dst = grouped[:].rearrange("p (c i) t -> p c t i", i=4)
+            src = raw[:, g, :, :].rearrange("p t (c i) -> p c t i", i=4)
+            split = vector_cols // 4
+            if vector_cols > 0:
+                nc.vector.tensor_copy(out=dst[:, :split], in_=src[:, :split])
+            nc.scalar.copy(out=dst[:, split:], in_=src[:, split:])
+            for bank in range(HD // BANK):
+                cols = slice(bank * BANK, (bank + 1) * BANK)
+                nc.vector.quantize_mx(
+                    out=w_codes[:, m, g, cols].bitcast(FP8X4),
+                    scales=w_scales[:, m, g, cols],
+                    in_=grouped[:, cols, :].rearrange("p c t -> p (c t)"),
+                )
+
+        def project_norm_rotate(n, stream, qk):
+            m = 2 * stream + qk
+            tokens = slice(n * P, (n + 1) * P)
+            y = work.tile([P, H, 2, PAIRS], F32, name="y")
+            for bank in range(HD // BANK):
+                cols = slice(bank * BANK, (bank + 1) * BANK)
+                acc = psum_y.tile([P, BANK], F32, name="acc")
+                for g in range(PASSES):
+                    nc.tensor.matmul_mx(
+                        out=acc[:],
+                        lhsT=act_codes[:, g, tokens].bitcast(FP8X4),
+                        lhsT_scale=act_scales[:, g, tokens],
+                        rhs=w_codes[:, m, g, cols].bitcast(FP8X4),
+                        rhs_scale=w_scales[:, m, g, cols],
+                        start=(g == 0),
+                        stop=(g == PASSES - 1),
+                    )
+                nc.vector.tensor_tensor(
+                    out=y[:, bank * BANK_HEADS : (bank + 1) * BANK_HEADS, :, :],
+                    in0=acc[:].rearrange("p (h i t) -> p h t i", h=BANK_HEADS, t=2),
+                    in1=bias_bc[:, m, cols].rearrange("p (h i t) -> p h t i", h=BANK_HEADS, t=2),
+                    op=ALU.add,
+                )
+
+            sumsq = work.tile([P, H], F32, name="sumsq")
+            for h in range(H):
+                squares = work.tile([P, D], BF16, name="squares")
+                nc.scalar.activation(
+                    out=squares[:],
+                    in_=y[:, h, :, :].rearrange("p t i -> p (t i)"),
+                    func=ACT.Square,
+                    accum_out=sumsq[:, h : h + 1],
+                )
+            rms = work.tile([P, H], F32, name="rms")
+            nc.scalar.activation(out=rms[:], in_=sumsq[:], func=ACT.Sqrt, bias=eps_col[:, 0:1], scale=1.0 / D)
+            inv_rms = work.tile([P, H], F32, name="inv_rms")
+            nc.vector.reciprocal(out=inv_rms[:], in_=rms[:])
+
+            same = work.tile([P, H, 2, PAIRS], F32, name="same")
+            nc.vector.tensor_tensor(
+                out=same[:].rearrange("p h t i -> p h (t i)"),
+                in0=y[:].rearrange("p h t i -> p h (t i)"),
+                in1=rot[:, n, qk, SAME, :].unsqueeze(1).to_broadcast([P, H, D]),
+                op=ALU.mult,
+            )
+            other = work.tile([P, H, 2, PAIRS], F32, name="other")
+            for t in range(2):
+                nc.vector.tensor_tensor(
+                    out=other[:, :, t, :],
+                    in0=y[:, :, 1 - t, :],
+                    in1=rot[:, n, qk, OTHER, t * PAIRS : (t + 1) * PAIRS].unsqueeze(1).to_broadcast([P, H, PAIRS]),
+                    op=ALU.mult,
+                )
+            nc.vector.tensor_tensor(out=same[:], in0=same[:], in1=other[:], op=ALU.add)
+
+            result = work.tile([P, H, PAIRS, 2], F32, name="result")
+            for h in range(H):
+                nc.scalar.activation(
+                    out=result[:, h, :, :],
+                    in_=same[:, h, :, :].rearrange("p t i -> p i t"),
+                    func=ACT.Copy,
+                    scale=inv_rms[:, h : h + 1],
+                )
+            tile_lo, tiles = ((TEXT_TILES, IMAGE_TILES), (0, TEXT_TILES))[stream]
+            out_rows = token_rows(outs[qk].rearrange("b s h d -> (b s) (h d)"), tile_lo, tiles)
+            nc.scalar.dma_start(out=out_rows[:, n - tile_lo, :], in_=result[:].rearrange("p h i t -> p (h i t)"))
+
+        for first_tile in range(TEXT_TILES, TOKEN_TILES, 2):
+            quantise_activations(first_tile)
+        for g in range(PASSES):
+            quantise_weight_pass(raw_q, 0, g, IMAGE_VECTOR_COLS)
+        raw_aq = load_weight(2)
+        for g in range(PASSES):
+            quantise_weight_pass(raw_k, 1, g, IMAGE_VECTOR_COLS)
+        raw_ak = load_weight(3)
+
+        for j in range(IMAGE_TILES):
+            for qk in range(2):
+                project_norm_rotate(TEXT_TILES + j, 0, qk)
+            if j == 0:
+                quantise_activations(0)
+            elif j <= 2:
+                quantise_weight_pass(raw_aq, 2, j - 1, 0)
+            elif j <= 4:
+                quantise_weight_pass(raw_ak, 3, j - 3, 0)
+        for n in range(TEXT_TILES):
+            for qk in range(2):
+                project_norm_rotate(n, 1, qk)

@@ -69,9 +69,10 @@ def tile_fluxjointattention_pa_kernel(
         keep = ctx.enter_context(tc.tile_pool(name="keep", bufs=1))
         raw_pool = ctx.enter_context(tc.tile_pool(name="raw", bufs=2))
         stage = ctx.enter_context(tc.tile_pool(name="stage", bufs=2))
-        work = ctx.enter_context(tc.tile_pool(name="work", bufs=3))
+        work = ctx.enter_context(tc.tile_pool(name="work", bufs=4))
         psum_t = ctx.enter_context(tc.psum_pool(name="psum_t", bufs=2))
-        psum_y = ctx.enter_context(tc.psum_pool(name="psum_y", bufs=6))
+        psum_rot = ctx.enter_context(tc.psum_pool(name="psum_rot", bufs=2))
+        psum_y = ctx.enter_context(tc.psum_pool(name="psum_y", bufs=4))
 
         act_sb = keep.tile([P, TOKEN_TILES, DM], BF16)
         nc.sync.dma_start(
@@ -187,7 +188,18 @@ def tile_fluxjointattention_pa_kernel(
                     in_=grouped[:, cols, :].rearrange("p c t -> p (c t)"),
                 )
 
-        def project_norm_rotate(n, stream, qk):
+        def tables_into_psum(n):
+            rot_ps = psum_rot.tile([P, 2, 2, D], F32, name="rot_ps")
+            nc.tensor.matmul(
+                out=rot_ps[:].rearrange("p q s d -> p (q s d)"),
+                lhsT=ident[:],
+                rhs=rot[:, n, :, :, :].rearrange("p q s d -> p (q s d)"),
+                start=True,
+                stop=True,
+            )
+            return rot_ps
+
+        def project_norm_rotate(n, stream, qk, rot_ps):
             m = 2 * stream + qk
             tokens = slice(n * P, (n + 1) * P)
             y = work.tile([P, H, 2, PAIRS], F32, name="y")
@@ -220,16 +232,16 @@ def tile_fluxjointattention_pa_kernel(
                     func=ACT.Square,
                     accum_out=sumsq[:, h : h + 1],
                 )
-            rms = work.tile([P, H], F32, name="rms")
-            nc.scalar.activation(out=rms[:], in_=sumsq[:], func=ACT.Sqrt, bias=eps_col[:, 0:1], scale=1.0 / D)
             inv_rms = work.tile([P, H], F32, name="inv_rms")
-            nc.vector.reciprocal(out=inv_rms[:], in_=rms[:])
+            nc.scalar.activation(
+                out=inv_rms[:], in_=sumsq[:], func=ACT.Abs_reciprocal_sqrt, bias=eps_col[:, 0:1], scale=1.0 / D
+            )
 
             same = work.tile([P, H, 2, PAIRS], F32, name="same")
             nc.vector.tensor_tensor(
                 out=same[:].rearrange("p h t i -> p h (t i)"),
                 in0=y[:].rearrange("p h t i -> p h (t i)"),
-                in1=rot[:, n, qk, SAME, :].unsqueeze(1).to_broadcast([P, H, D]),
+                in1=rot_ps[:, qk, SAME, :].unsqueeze(1).to_broadcast([P, H, D]),
                 op=ALU.mult,
             )
             other = work.tile([P, H, 2, PAIRS], F32, name="other")
@@ -237,10 +249,10 @@ def tile_fluxjointattention_pa_kernel(
                 nc.vector.tensor_tensor(
                     out=other[:, :, t, :],
                     in0=y[:, :, 1 - t, :],
-                    in1=rot[:, n, qk, OTHER, t * PAIRS : (t + 1) * PAIRS].unsqueeze(1).to_broadcast([P, H, PAIRS]),
+                    in1=rot_ps[:, qk, OTHER, t * PAIRS : (t + 1) * PAIRS].unsqueeze(1).to_broadcast([P, H, PAIRS]),
                     op=ALU.mult,
                 )
-            nc.vector.tensor_tensor(out=same[:], in0=same[:], in1=other[:], op=ALU.add)
+            nc.gpsimd.tensor_tensor(out=same[:], in0=same[:], in1=other[:], op=ALU.add)
 
             result = work.tile([P, H, PAIRS, 2], F32, name="result")
             for h in range(H):
@@ -264,8 +276,9 @@ def tile_fluxjointattention_pa_kernel(
         raw_ak = load_weight(3)
 
         for j in range(IMAGE_TILES):
+            rot_ps = tables_into_psum(TEXT_TILES + j)
             for qk in range(2):
-                project_norm_rotate(TEXT_TILES + j, 0, qk)
+                project_norm_rotate(TEXT_TILES + j, 0, qk, rot_ps)
             if j == 0:
                 quantise_activations(0)
             elif j <= 2:
@@ -273,5 +286,6 @@ def tile_fluxjointattention_pa_kernel(
             elif j <= 4:
                 quantise_weight_pass(raw_ak, 3, j - 3, 0)
         for n in range(TEXT_TILES):
+            rot_ps = tables_into_psum(n)
             for qk in range(2):
-                project_norm_rotate(n, 1, qk)
+                project_norm_rotate(n, 1, qk, rot_ps)

@@ -7,6 +7,7 @@ F32 = mybir.dt.float32
 BF16 = mybir.dt.bfloat16
 U32 = mybir.dt.uint32
 U8 = mybir.dt.uint8
+I32 = mybir.dt.int32
 FP8X4 = mybir.dt.float8_e4m3fn_x4
 ALU = mybir.AluOpType
 ACT = mybir.ActivationFunctionType
@@ -27,7 +28,7 @@ EPS = 1e-6
 TEXT_TILES = 2
 IMAGE_TILES = 6
 TOKEN_TILES = TEXT_TILES + IMAGE_TILES
-TEXT_ROWS = TEXT_TILES * P
+STREAM_TILES = ((TEXT_TILES, IMAGE_TILES), (0, TEXT_TILES))
 
 IMAGE_VECTOR_COLS = 640
 
@@ -69,16 +70,23 @@ def tile_fluxjointattention_pa_kernel(
         keep = ctx.enter_context(tc.tile_pool(name="keep", bufs=1))
         raw_pool = ctx.enter_context(tc.tile_pool(name="raw", bufs=2))
         stage = ctx.enter_context(tc.tile_pool(name="stage", bufs=2))
-        work = ctx.enter_context(tc.tile_pool(name="work", bufs=4))
+        work = ctx.enter_context(tc.tile_pool(name="work", bufs=3))
         psum_t = ctx.enter_context(tc.psum_pool(name="psum_t", bufs=2))
         psum_rot = ctx.enter_context(tc.psum_pool(name="psum_rot", bufs=2))
         psum_y = ctx.enter_context(tc.psum_pool(name="psum_y", bufs=4))
 
+        rows = keep.tile([P, 4 * D + 4 * HD], BF16)
+        nc.vector.memset(rows[:].bitcast(I32), 0)
         act_sb = keep.tile([P, TOKEN_TILES, DM], BF16)
-        nc.sync.dma_start(
-            out=act_sb[:, TEXT_TILES:, :],
-            in_=hidden_states.rearrange("b (p n) k -> p (b n) k", n=IMAGE_TILES),
-        )
+        cos_sb = keep.tile([P, TOKEN_TILES, D], BF16)
+        sin_sb = keep.tile([P, TOKEN_TILES, D], BF16)
+        image_rows = hidden_states.rearrange("b (p n) k -> p (b n) k", n=IMAGE_TILES)
+        text_rows = encoder_hidden_states.rearrange("b (p n) k -> p (b n) k", n=TEXT_TILES)
+
+        def load_bias(m):
+            nc.sync.dma_start(
+                out=rows[0:1, 4 * D + m * HD : 4 * D + (m + 1) * HD], in_=biases[m].unsqueeze(0)
+            )
 
         def load_weight(m):
             raw = raw_pool.tile([P, PASSES, PACK, HD], BF16, name="raw")
@@ -91,40 +99,57 @@ def tile_fluxjointattention_pa_kernel(
                 )
             return raw
 
+        for m in range(4):
+            nc.sync.dma_start(out=rows[0:1, m * D : (m + 1) * D], in_=gains[m].unsqueeze(0))
+        nc.sync.dma_start(out=cos_sb[:, TEXT_TILES:, :], in_=token_rows(rope_cos, TEXT_TILES, IMAGE_TILES))
+        nc.sync.dma_start(out=sin_sb[:, TEXT_TILES:, :], in_=token_rows(rope_sin, TEXT_TILES, IMAGE_TILES))
+        nc.sync.dma_start(out=act_sb[:, TEXT_TILES : TEXT_TILES + 2, :], in_=image_rows[:, :2, :])
         raw_q = load_weight(0)
+        load_bias(0)
+        load_bias(1)
+        nc.sync.dma_start(out=act_sb[:, TEXT_TILES + 2 :, :], in_=image_rows[:, 2:, :])
         raw_k = load_weight(1)
-        nc.sync.dma_start(
-            out=act_sb[:, :TEXT_TILES, :],
-            in_=encoder_hidden_states.rearrange("b (p n) k -> p (b n) k", n=TEXT_TILES),
-        )
-
-        cos_sb = keep.tile([P, TOKEN_TILES, D], BF16)
-        sin_sb = keep.tile([P, TOKEN_TILES, D], BF16)
-        gain_bc = keep.tile([P, 4, D], BF16)
-        bias_bc = keep.tile([P, 4, HD], BF16)
-        for table_sb, table in ((cos_sb, rope_cos), (sin_sb, rope_sin)):
-            nc.scalar.dma_start(
-                out=table_sb[:, TEXT_TILES:, :], in_=token_rows(table, TEXT_TILES, IMAGE_TILES)
-            )
-            nc.scalar.dma_start(out=table_sb[:, :TEXT_TILES, :], in_=token_rows(table, 0, TEXT_TILES))
-        for m in range(4):
-            nc.scalar.dma_start(out=gain_bc[:, m, :], in_=gains[m].partition_broadcast(P))
-        for m in range(4):
-            nc.gpsimd.dma_start(out=bias_bc[:, m, :], in_=biases[m].partition_broadcast(P))
+        nc.sync.dma_start(out=act_sb[:, :TEXT_TILES, :], in_=text_rows)
+        nc.sync.dma_start(out=cos_sb[:, :TEXT_TILES, :], in_=token_rows(rope_cos, 0, TEXT_TILES))
+        nc.sync.dma_start(out=sin_sb[:, :TEXT_TILES, :], in_=token_rows(rope_sin, 0, TEXT_TILES))
+        load_bias(2)
+        load_bias(3)
 
         ident = keep.tile([P, P], F32)
         make_identity(nc, ident[:])
         eps_col = keep.tile([P, 1], F32)
         nc.vector.memset(eps_col[:], EPS)
+        ones = keep.tile([P, P], BF16)
+        nc.vector.memset(ones[:], 1.0)
 
-        gain_pairs = gain_bc[:].rearrange("p m (i t) -> p m i t", t=2)
-        gain_other = keep.tile([P, 4, 2, PAIRS], BF16)
+        def spread(col_lo):
+            bank = psum_y.tile([P, BANK], F32, name="acc")
+            nc.tensor.matmul(out=bank[:], lhsT=ones[:], rhs=rows[:, col_lo : col_lo + BANK], start=True, stop=True)
+            return bank
+
+        bias_bc = keep.tile([P, 4, H, 2, PAIRS], BF16)
+
+        def spread_bias(m):
+            for bank in range(HD // BANK):
+                nc.scalar.copy(
+                    out=bias_bc[:, m, bank * BANK_HEADS : (bank + 1) * BANK_HEADS, :, :],
+                    in_=spread(4 * D + m * HD + bank * BANK)[:].rearrange(
+                        "p (h i t) -> p h t i", h=BANK_HEADS, t=2
+                    ),
+                )
+
+        gain_pairs = spread(0)[:].rearrange("p (m i t) -> p m i t", m=4, t=2)
+        gain_same = keep.tile([P, 4, 2, PAIRS], F32)
+        gain_other = keep.tile([P, 4, 2, PAIRS], F32)
+        nc.vector.tensor_copy(out=gain_same[:], in_=gain_pairs.rearrange("p m i t -> p m t i"))
         nc.vector.tensor_scalar_mul(out=gain_other[:, :, 0, :], in0=gain_pairs[:, :, :, 1], scalar1=-1.0)
         nc.vector.tensor_copy(out=gain_other[:, :, 1, :], in_=gain_pairs[:, :, :, 0])
 
         SAME, OTHER = 0, 1
         rot = keep.tile([P, TOKEN_TILES, 2, 2, D], F32)
-        for stream, (tile_lo, tiles) in enumerate(((TEXT_TILES, IMAGE_TILES), (0, TEXT_TILES))):
+
+        def build_tables(stream):
+            tile_lo, tiles = STREAM_TILES[stream]
             tile_range = slice(tile_lo, tile_lo + tiles)
             shape = [P, tiles, 2, PAIRS]
             for qk in range(2):
@@ -132,7 +157,7 @@ def tile_fluxjointattention_pa_kernel(
                 nc.vector.tensor_tensor(
                     out=rot[:, tile_range, qk, SAME, :].rearrange("p n (t i) -> p n t i", t=2),
                     in0=cos_sb[:, tile_range, :].rearrange("p n (i t) -> p n t i", t=2),
-                    in1=gain_bc[:, m, :].rearrange("p (i t) -> p t i", t=2).unsqueeze(1).to_broadcast(shape),
+                    in1=gain_same[:, m, :, :].unsqueeze(1).to_broadcast(shape),
                     op=ALU.mult,
                 )
                 nc.vector.tensor_tensor(
@@ -219,7 +244,7 @@ def tile_fluxjointattention_pa_kernel(
                 nc.vector.tensor_tensor(
                     out=y[:, bank * BANK_HEADS : (bank + 1) * BANK_HEADS, :, :],
                     in0=acc[:].rearrange("p (h i t) -> p h t i", h=BANK_HEADS, t=2),
-                    in1=bias_bc[:, m, cols].rearrange("p (h i t) -> p h t i", h=BANK_HEADS, t=2),
+                    in1=bias_bc[:, m, bank * BANK_HEADS : (bank + 1) * BANK_HEADS, :, :],
                     op=ALU.add,
                 )
 
@@ -237,7 +262,7 @@ def tile_fluxjointattention_pa_kernel(
                 out=inv_rms[:], in_=sumsq[:], func=ACT.Abs_reciprocal_sqrt, bias=eps_col[:, 0:1], scale=1.0 / D
             )
 
-            same = work.tile([P, H, 2, PAIRS], F32, name="same")
+            same = work.tile([P, H, 2, PAIRS], F32, name="same", bufs=4)
             nc.vector.tensor_tensor(
                 out=same[:].rearrange("p h t i -> p h (t i)"),
                 in0=y[:].rearrange("p h t i -> p h (t i)"),
@@ -262,14 +287,18 @@ def tile_fluxjointattention_pa_kernel(
                     func=ACT.Copy,
                     scale=inv_rms[:, h : h + 1],
                 )
-            tile_lo, tiles = ((TEXT_TILES, IMAGE_TILES), (0, TEXT_TILES))[stream]
+            tile_lo, tiles = STREAM_TILES[stream]
             out_rows = token_rows(outs[qk].rearrange("b s h d -> (b s) (h d)"), tile_lo, tiles)
             nc.scalar.dma_start(out=out_rows[:, n - tile_lo, :], in_=result[:].rearrange("p h i t -> p (h i t)"))
 
-        for first_tile in range(TEXT_TILES, TOKEN_TILES, 2):
-            quantise_activations(first_tile)
+        build_tables(0)
+        quantise_activations(TEXT_TILES)
         for g in range(PASSES):
             quantise_weight_pass(raw_q, 0, g, IMAGE_VECTOR_COLS)
+        spread_bias(0)
+        spread_bias(1)
+        for first_tile in range(TEXT_TILES + 2, TOKEN_TILES, 2):
+            quantise_activations(first_tile)
         raw_aq = load_weight(2)
         for g in range(PASSES):
             quantise_weight_pass(raw_k, 1, g, IMAGE_VECTOR_COLS)
@@ -281,6 +310,9 @@ def tile_fluxjointattention_pa_kernel(
                 project_norm_rotate(TEXT_TILES + j, 0, qk, rot_ps)
             if j == 0:
                 quantise_activations(0)
+                build_tables(1)
+                spread_bias(2)
+                spread_bias(3)
             elif j <= 2:
                 quantise_weight_pass(raw_aq, 2, j - 1, 0)
             elif j <= 4:

@@ -30,7 +30,7 @@ IMAGE_TILES = 6
 TOKEN_TILES = TEXT_TILES + IMAGE_TILES
 STREAM_TILES = ((TEXT_TILES, IMAGE_TILES), (0, TEXT_TILES))
 
-IMAGE_VECTOR_COLS = 640
+FIRST_WEIGHT_VECTOR_COLS = 640
 
 FLOPS = 2 * (TOKEN_TILES * P) * DM * (2 * HD)
 
@@ -197,14 +197,23 @@ def tile_fluxjointattention_pa_kernel(
         w_codes = keep.tile([P, 4, PASSES, HD], U32, align_bytes=64)
         w_scales = keep.tile([P, 4, PASSES, HD], U8, align_bytes=64)
 
-        def quantise_weight_pass(raw, m, g, vector_cols):
+        def quantise_weight_pass(raw, m, g):
             grouped = stage.tile([P, HD, PACK], BF16, name="w_grouped", align_bytes=64)
             dst = grouped[:].rearrange("p (c i) t -> p c t i", i=4)
             src = raw[:, g, :, :].rearrange("p t (c i) -> p c t i", i=4)
-            split = vector_cols // 4
-            if vector_cols > 0:
+            runs = HD // 4
+            if m == 0:
+                split = FIRST_WEIGHT_VECTOR_COLS // 4
                 nc.vector.tensor_copy(out=dst[:, :split], in_=src[:, :split])
-            nc.scalar.copy(out=dst[:, split:], in_=src[:, split:])
+                nc.scalar.copy(out=dst[:, split:], in_=src[:, split:])
+            else:
+                for half in (slice(0, runs // 2), slice(runs // 2, runs)):
+                    if m == 1:
+                        nc.scalar.copy(out=dst[:, half], in_=src[:, half])
+                    else:
+                        nc.gpsimd.tensor_scalar(
+                            out=dst[:, half], in0=src[:, half], scalar1=1.0, scalar2=0.0, op0=ALU.mult, op1=ALU.add
+                        )
             for bank in range(HD // BANK):
                 cols = slice(bank * BANK, (bank + 1) * BANK)
                 nc.vector.quantize_mx(
@@ -213,19 +222,16 @@ def tile_fluxjointattention_pa_kernel(
                     in_=grouped[:, cols, :].rearrange("p c t -> p (c t)"),
                 )
 
-        def tables_into_psum(n):
-            rot_ps = psum_rot.tile([P, 2, 2, D], F32, name="rot_ps")
+        def project_norm_rotate(n, stream, qk):
+            m = 2 * stream + qk
+            rot_ps = psum_rot.tile([P, 2, D], F32, name="rot_ps")
             nc.tensor.matmul(
-                out=rot_ps[:].rearrange("p q s d -> p (q s d)"),
+                out=rot_ps[:].rearrange("p s d -> p (s d)"),
                 lhsT=ident[:],
-                rhs=rot[:, n, :, :, :].rearrange("p q s d -> p (q s d)"),
+                rhs=rot[:, n, qk, :, :].rearrange("p s d -> p (s d)"),
                 start=True,
                 stop=True,
             )
-            return rot_ps
-
-        def project_norm_rotate(n, stream, qk, rot_ps):
-            m = 2 * stream + qk
             tokens = slice(n * P, (n + 1) * P)
             y = work.tile([P, H, 2, PAIRS], F32, name="y")
             for bank in range(HD // BANK):
@@ -266,7 +272,7 @@ def tile_fluxjointattention_pa_kernel(
             nc.vector.tensor_tensor(
                 out=same[:].rearrange("p h t i -> p h (t i)"),
                 in0=y[:].rearrange("p h t i -> p h (t i)"),
-                in1=rot_ps[:, qk, SAME, :].unsqueeze(1).to_broadcast([P, H, D]),
+                in1=rot_ps[:, SAME, :].unsqueeze(1).to_broadcast([P, H, D]),
                 op=ALU.mult,
             )
             other = work.tile([P, H, 2, PAIRS], F32, name="other")
@@ -274,7 +280,7 @@ def tile_fluxjointattention_pa_kernel(
                 nc.vector.tensor_tensor(
                     out=other[:, :, t, :],
                     in0=y[:, :, 1 - t, :],
-                    in1=rot_ps[:, qk, OTHER, t * PAIRS : (t + 1) * PAIRS].unsqueeze(1).to_broadcast([P, H, PAIRS]),
+                    in1=rot_ps[:, OTHER, t * PAIRS : (t + 1) * PAIRS].unsqueeze(1).to_broadcast([P, H, PAIRS]),
                     op=ALU.mult,
                 )
             nc.gpsimd.tensor_tensor(out=same[:], in0=same[:], in1=other[:], op=ALU.add)
@@ -294,30 +300,33 @@ def tile_fluxjointattention_pa_kernel(
         build_tables(0)
         quantise_activations(TEXT_TILES)
         for g in range(PASSES):
-            quantise_weight_pass(raw_q, 0, g, IMAGE_VECTOR_COLS)
+            quantise_weight_pass(raw_q, 0, g)
         spread_bias(0)
-        spread_bias(1)
-        for first_tile in range(TEXT_TILES + 2, TOKEN_TILES, 2):
-            quantise_activations(first_tile)
         raw_aq = load_weight(2)
-        for g in range(PASSES):
-            quantise_weight_pass(raw_k, 1, g, IMAGE_VECTOR_COLS)
+
+        for j in range(IMAGE_TILES):
+            project_norm_rotate(TEXT_TILES + j, 0, 0)
+            if j == 0:
+                quantise_activations(TEXT_TILES + 2)
+                quantise_activations(TEXT_TILES + 4)
+            elif j <= 2:
+                quantise_weight_pass(raw_k, 1, j - 1)
+            elif j == 3:
+                spread_bias(1)
+                quantise_activations(0)
+            else:
+                quantise_weight_pass(raw_aq, 2, j - 4)
         raw_ak = load_weight(3)
 
         for j in range(IMAGE_TILES):
-            rot_ps = tables_into_psum(TEXT_TILES + j)
-            for qk in range(2):
-                project_norm_rotate(TEXT_TILES + j, 0, qk, rot_ps)
+            project_norm_rotate(TEXT_TILES + j, 0, 1)
             if j == 0:
-                quantise_activations(0)
                 build_tables(1)
                 spread_bias(2)
                 spread_bias(3)
             elif j <= 2:
-                quantise_weight_pass(raw_aq, 2, j - 1, 0)
-            elif j <= 4:
-                quantise_weight_pass(raw_ak, 3, j - 3, 0)
-        for n in range(TEXT_TILES):
-            rot_ps = tables_into_psum(n)
-            for qk in range(2):
-                project_norm_rotate(n, 1, qk, rot_ps)
+                quantise_weight_pass(raw_ak, 3, j - 1)
+
+        for qk in range(2):
+            for n in range(TEXT_TILES):
+                project_norm_rotate(n, 1, qk)

@@ -30,7 +30,7 @@ IMAGE_TILES = 6
 TOKEN_TILES = TEXT_TILES + IMAGE_TILES
 STREAM_TILES = ((TEXT_TILES, IMAGE_TILES), (0, TEXT_TILES))
 
-FIRST_WEIGHT_VECTOR_COLS = 640
+VECTOR_COLS = 512
 
 FLOPS = 2 * (TOKEN_TILES * P) * DM * (2 * HD)
 
@@ -101,11 +101,11 @@ def tile_fluxjointattention_pa_kernel(
 
         for m in range(4):
             nc.sync.dma_start(out=rows[0:1, m * D : (m + 1) * D], in_=gains[m].unsqueeze(0))
+        load_bias(0)
         nc.sync.dma_start(out=cos_sb[:, TEXT_TILES:, :], in_=token_rows(rope_cos, TEXT_TILES, IMAGE_TILES))
         nc.sync.dma_start(out=sin_sb[:, TEXT_TILES:, :], in_=token_rows(rope_sin, TEXT_TILES, IMAGE_TILES))
         nc.sync.dma_start(out=act_sb[:, TEXT_TILES : TEXT_TILES + 2, :], in_=image_rows[:, :2, :])
         raw_q = load_weight(0)
-        load_bias(0)
         load_bias(1)
         nc.sync.dma_start(out=act_sb[:, TEXT_TILES + 2 :, :], in_=image_rows[:, 2:, :])
         raw_k = load_weight(1)
@@ -201,19 +201,9 @@ def tile_fluxjointattention_pa_kernel(
             grouped = stage.tile([P, HD, PACK], BF16, name="w_grouped", align_bytes=64)
             dst = grouped[:].rearrange("p (c i) t -> p c t i", i=4)
             src = raw[:, g, :, :].rearrange("p t (c i) -> p c t i", i=4)
-            runs = HD // 4
-            if m == 0:
-                split = FIRST_WEIGHT_VECTOR_COLS // 4
-                nc.vector.tensor_copy(out=dst[:, :split], in_=src[:, :split])
-                nc.scalar.copy(out=dst[:, split:], in_=src[:, split:])
-            else:
-                for half in (slice(0, runs // 2), slice(runs // 2, runs)):
-                    if m == 1:
-                        nc.scalar.copy(out=dst[:, half], in_=src[:, half])
-                    else:
-                        nc.gpsimd.tensor_scalar(
-                            out=dst[:, half], in0=src[:, half], scalar1=1.0, scalar2=0.0, op0=ALU.mult, op1=ALU.add
-                        )
+            split = VECTOR_COLS // 4
+            nc.vector.tensor_copy(out=dst[:, :split], in_=src[:, :split])
+            nc.scalar.copy(out=dst[:, split:], in_=src[:, split:])
             for bank in range(HD // BANK):
                 cols = slice(bank * BANK, (bank + 1) * BANK)
                 nc.vector.quantize_mx(
@@ -222,7 +212,13 @@ def tile_fluxjointattention_pa_kernel(
                     in_=grouped[:, cols, :].rearrange("p c t -> p (c t)"),
                 )
 
-        def project_norm_rotate(n, stream, qk):
+        units = [(TEXT_TILES + j, 0, qk) for qk in range(2) for j in range(IMAGE_TILES)]
+        units += [(n, 1, qk) for qk in range(2) for n in range(TEXT_TILES)]
+        in_psum = {}
+        in_sbuf = {}
+
+        def multiply(u):
+            n, stream, qk = units[u]
             m = 2 * stream + qk
             rot_ps = psum_rot.tile([P, 2, D], F32, name="rot_ps")
             nc.tensor.matmul(
@@ -233,7 +229,7 @@ def tile_fluxjointattention_pa_kernel(
                 stop=True,
             )
             tokens = slice(n * P, (n + 1) * P)
-            y = work.tile([P, H, 2, PAIRS], F32, name="y")
+            banks = []
             for bank in range(HD // BANK):
                 cols = slice(bank * BANK, (bank + 1) * BANK)
                 acc = psum_y.tile([P, BANK], F32, name="acc")
@@ -247,14 +243,23 @@ def tile_fluxjointattention_pa_kernel(
                         start=(g == 0),
                         stop=(g == PASSES - 1),
                     )
+                banks.append(acc)
+            in_psum[u] = (rot_ps, banks)
+
+        def bias_squares_products(u):
+            n, stream, qk = units[u]
+            m = 2 * stream + qk
+            rot_ps, banks = in_psum[u]
+            y = work.tile([P, H, 2, PAIRS], F32, name="y")
+            for bank in range(HD // BANK):
+                heads = slice(bank * BANK_HEADS, (bank + 1) * BANK_HEADS)
                 nc.vector.tensor_tensor(
-                    out=y[:, bank * BANK_HEADS : (bank + 1) * BANK_HEADS, :, :],
-                    in0=acc[:].rearrange("p (h i t) -> p h t i", h=BANK_HEADS, t=2),
-                    in1=bias_bc[:, m, bank * BANK_HEADS : (bank + 1) * BANK_HEADS, :, :],
+                    out=y[:, heads, :, :],
+                    in0=banks[bank][:].rearrange("p (h i t) -> p h t i", h=BANK_HEADS, t=2),
+                    in1=bias_bc[:, m, heads, :, :],
                     op=ALU.add,
                 )
-
-            sumsq = work.tile([P, H], F32, name="sumsq")
+            sumsq = work.tile([P, H], F32, name="sumsq", bufs=4)
             for h in range(H):
                 squares = work.tile([P, D], BF16, name="squares")
                 nc.scalar.activation(
@@ -263,11 +268,10 @@ def tile_fluxjointattention_pa_kernel(
                     func=ACT.Square,
                     accum_out=sumsq[:, h : h + 1],
                 )
-            inv_rms = work.tile([P, H], F32, name="inv_rms")
+            inv_rms = work.tile([P, H], F32, name="inv_rms", bufs=4)
             nc.scalar.activation(
                 out=inv_rms[:], in_=sumsq[:], func=ACT.Abs_reciprocal_sqrt, bias=eps_col[:, 0:1], scale=1.0 / D
             )
-
             same = work.tile([P, H, 2, PAIRS], F32, name="same", bufs=4)
             nc.vector.tensor_tensor(
                 out=same[:].rearrange("p h t i -> p h (t i)"),
@@ -276,15 +280,35 @@ def tile_fluxjointattention_pa_kernel(
                 op=ALU.mult,
             )
             other = work.tile([P, H, 2, PAIRS], F32, name="other")
-            for t in range(2):
-                nc.vector.tensor_tensor(
-                    out=other[:, :, t, :],
-                    in0=y[:, :, 1 - t, :],
-                    in1=rot_ps[:, OTHER, t * PAIRS : (t + 1) * PAIRS].unsqueeze(1).to_broadcast([P, H, PAIRS]),
+            nc.vector.tensor_tensor(
+                out=other[:, :, 0, :],
+                in0=y[:, :, 1, :],
+                in1=rot_ps[:, OTHER, :PAIRS].unsqueeze(1).to_broadcast([P, H, PAIRS]),
+                op=ALU.mult,
+            )
+            if stream == 0:
+                nc.gpsimd.tensor_tensor(
+                    out=other[:, :, 1, :],
+                    in0=y[:, :, 0, :],
+                    in1=rot[:, n, qk, OTHER, PAIRS:].unsqueeze(1).to_broadcast([P, H, PAIRS]),
                     op=ALU.mult,
                 )
+            else:
+                nc.vector.tensor_tensor(
+                    out=other[:, :, 1, :],
+                    in0=y[:, :, 0, :],
+                    in1=rot_ps[:, OTHER, PAIRS:].unsqueeze(1).to_broadcast([P, H, PAIRS]),
+                    op=ALU.mult,
+                )
+            in_sbuf[u] = (same, other, inv_rms)
+
+        def add_products(u):
+            same, other, inv_rms = in_sbuf[u]
             nc.gpsimd.tensor_tensor(out=same[:], in0=same[:], in1=other[:], op=ALU.add)
 
+        def normalise_store(u):
+            n, stream, qk = units[u]
+            same, other, inv_rms = in_sbuf[u]
             result = work.tile([P, H, PAIRS, 2], F32, name="result")
             for h in range(H):
                 nc.scalar.activation(
@@ -302,31 +326,32 @@ def tile_fluxjointattention_pa_kernel(
         for g in range(PASSES):
             quantise_weight_pass(raw_q, 0, g)
         spread_bias(0)
-        raw_aq = load_weight(2)
+        raws = {1: raw_k, 2: load_weight(2)}
 
-        for j in range(IMAGE_TILES):
-            project_norm_rotate(TEXT_TILES + j, 0, 0)
-            if j == 0:
+        multiply(0)
+        for s in range(len(units) + 2):
+            if s + 1 < len(units):
+                multiply(s + 1)
+            if 1 <= s <= len(units):
+                add_products(s - 1)
+            if s >= 2:
+                normalise_store(s - 2)
+            if s < len(units):
+                bias_squares_products(s)
+            if s == 0:
                 quantise_activations(TEXT_TILES + 2)
                 quantise_activations(TEXT_TILES + 4)
-            elif j <= 2:
-                quantise_weight_pass(raw_k, 1, j - 1)
-            elif j == 3:
+            elif s <= 2:
+                quantise_weight_pass(raws[1], 1, s - 1)
+            elif s == 3:
+                raws[3] = load_weight(3)
                 spread_bias(1)
                 quantise_activations(0)
-            else:
-                quantise_weight_pass(raw_aq, 2, j - 4)
-        raw_ak = load_weight(3)
-
-        for j in range(IMAGE_TILES):
-            project_norm_rotate(TEXT_TILES + j, 0, 1)
-            if j == 0:
+            elif s <= 5:
+                quantise_weight_pass(raws[2], 2, s - 4)
+            elif s == 6:
                 build_tables(1)
                 spread_bias(2)
                 spread_bias(3)
-            elif j <= 2:
-                quantise_weight_pass(raw_ak, 3, j - 1)
-
-        for qk in range(2):
-            for n in range(TEXT_TILES):
-                project_norm_rotate(n, 1, qk)
+            elif s <= 8:
+                quantise_weight_pass(raws[3], 3, s - 7)

from contextlib import ExitStack

import concourse.mybir as mybir
from concourse.masks import make_identity

F32 = mybir.dt.float32
BF16 = mybir.dt.bfloat16
U32 = mybir.dt.uint32
U8 = mybir.dt.uint8
I32 = mybir.dt.int32
FP8X4 = mybir.dt.float8_e4m3fn_x4
ALU = mybir.AluOpType
ACT = mybir.ActivationFunctionType

P = 128
PACK = 4
K_PASS = P * PACK
DM = 1024
PASSES = DM // K_PASS
H = 8
D = 128
PAIRS = D // 2
HD = H * D
BANK = 512
BANK_HEADS = BANK // D
EPS = 1e-6

TEXT_TILES = 2
IMAGE_TILES = 6
TOKEN_TILES = TEXT_TILES + IMAGE_TILES
STREAM_TILES = ((TEXT_TILES, IMAGE_TILES), (0, TEXT_TILES))

VECTOR_COLS = 512

FLOPS = 2 * (TOKEN_TILES * P) * DM * (2 * HD)


def tile_fluxjointattention_pa_kernel(
    tc,
    hidden_states,
    encoder_hidden_states,
    rope_cos,
    rope_sin,
    Wq,
    Wk,
    Waq,
    Wak,
    bq,
    bk,
    baq,
    bak,
    g_q,
    g_k,
    g_aq,
    g_ak,
    out_0,
    out_1,
):
    nc = tc.nc
    weights = (Wq, Wk, Waq, Wak)
    biases = (bq, bk, baq, bak)
    gains = (g_q, g_k, g_aq, g_ak)
    outs = (out_0, out_1)

    def token_rows(dram_rows, tile_lo, tiles):
        rows = dram_rows[tile_lo * P : (tile_lo + tiles) * P, :]
        return rows.rearrange("(p n) c -> p n c", n=tiles)

    with ExitStack() as ctx:
        keep = ctx.enter_context(tc.tile_pool(name="keep", bufs=1))
        raw_pool = ctx.enter_context(tc.tile_pool(name="raw", bufs=2))
        stage = ctx.enter_context(tc.tile_pool(name="stage", bufs=2))
        work = ctx.enter_context(tc.tile_pool(name="work", bufs=3))
        psum_t = ctx.enter_context(tc.psum_pool(name="psum_t", bufs=2))
        psum_rot = ctx.enter_context(tc.psum_pool(name="psum_rot", bufs=2))
        psum_y = ctx.enter_context(tc.psum_pool(name="psum_y", bufs=4))

        rows = keep.tile([P, 4 * D + 4 * HD], BF16)
        nc.vector.memset(rows[:].bitcast(I32), 0)
        act_sb = keep.tile([P, TOKEN_TILES, DM], BF16)
        cos_sb = keep.tile([P, TOKEN_TILES, D], BF16)
        sin_sb = keep.tile([P, TOKEN_TILES, D], BF16)
        image_rows = hidden_states.rearrange("b (p n) k -> p (b n) k", n=IMAGE_TILES)
        text_rows = encoder_hidden_states.rearrange("b (p n) k -> p (b n) k", n=TEXT_TILES)

        def load_bias(m):
            nc.sync.dma_start(
                out=rows[0:1, 4 * D + m * HD : 4 * D + (m + 1) * HD], in_=biases[m].unsqueeze(0)
            )

        def load_weight(m):
            raw = raw_pool.tile([P, PASSES, PACK, HD], BF16, name="raw")
            for g in range(PASSES):
                nc.sync.dma_start(
                    out=raw[:, g, :, :].rearrange("p (u e) n -> p u (e n)", e=2),
                    in_=weights[m][g * K_PASS : (g + 1) * K_PASS, :].rearrange(
                        "(u q e) n -> q u (e n)", u=2, e=2
                    ),
                )
            return raw

        for m in range(4):
            nc.sync.dma_start(out=rows[0:1, m * D : (m + 1) * D], in_=gains[m].unsqueeze(0))
        load_bias(0)
        nc.sync.dma_start(out=cos_sb[:, TEXT_TILES:, :], in_=token_rows(rope_cos, TEXT_TILES, IMAGE_TILES))
        nc.sync.dma_start(out=sin_sb[:, TEXT_TILES:, :], in_=token_rows(rope_sin, TEXT_TILES, IMAGE_TILES))
        nc.sync.dma_start(out=act_sb[:, TEXT_TILES : TEXT_TILES + 2, :], in_=image_rows[:, :2, :])
        raw_q = load_weight(0)
        load_bias(1)
        nc.sync.dma_start(out=act_sb[:, TEXT_TILES + 2 :, :], in_=image_rows[:, 2:, :])
        raw_k = load_weight(1)
        nc.sync.dma_start(out=act_sb[:, :TEXT_TILES, :], in_=text_rows)
        nc.sync.dma_start(out=cos_sb[:, :TEXT_TILES, :], in_=token_rows(rope_cos, 0, TEXT_TILES))
        nc.sync.dma_start(out=sin_sb[:, :TEXT_TILES, :], in_=token_rows(rope_sin, 0, TEXT_TILES))
        load_bias(2)
        load_bias(3)

        ident = keep.tile([P, P], F32)
        make_identity(nc, ident[:])
        eps_col = keep.tile([P, 1], F32)
        nc.vector.memset(eps_col[:], EPS)
        ones = keep.tile([P, P], BF16)
        nc.vector.memset(ones[:], 1.0)

        def spread(col_lo):
            bank = psum_y.tile([P, BANK], F32, name="acc")
            nc.tensor.matmul(out=bank[:], lhsT=ones[:], rhs=rows[:, col_lo : col_lo + BANK], start=True, stop=True)
            return bank

        bias_bc = keep.tile([P, 4, H, 2, PAIRS], BF16)

        def spread_bias(m):
            for bank in range(HD // BANK):
                nc.scalar.copy(
                    out=bias_bc[:, m, bank * BANK_HEADS : (bank + 1) * BANK_HEADS, :, :],
                    in_=spread(4 * D + m * HD + bank * BANK)[:].rearrange(
                        "p (h i t) -> p h t i", h=BANK_HEADS, t=2
                    ),
                )

        gain_pairs = spread(0)[:].rearrange("p (m i t) -> p m i t", m=4, t=2)
        gain_same = keep.tile([P, 4, 2, PAIRS], F32)
        gain_other = keep.tile([P, 4, 2, PAIRS], F32)
        nc.vector.tensor_copy(out=gain_same[:], in_=gain_pairs.rearrange("p m i t -> p m t i"))
        nc.vector.tensor_scalar_mul(out=gain_other[:, :, 0, :], in0=gain_pairs[:, :, :, 1], scalar1=-1.0)
        nc.vector.tensor_copy(out=gain_other[:, :, 1, :], in_=gain_pairs[:, :, :, 0])

        SAME, OTHER = 0, 1
        rot = keep.tile([P, TOKEN_TILES, 2, 2, D], F32)

        def build_tables(stream):
            tile_lo, tiles = STREAM_TILES[stream]
            tile_range = slice(tile_lo, tile_lo + tiles)
            shape = [P, tiles, 2, PAIRS]
            for qk in range(2):
                m = 2 * stream + qk
                nc.vector.tensor_tensor(
                    out=rot[:, tile_range, qk, SAME, :].rearrange("p n (t i) -> p n t i", t=2),
                    in0=cos_sb[:, tile_range, :].rearrange("p n (i t) -> p n t i", t=2),
                    in1=gain_same[:, m, :, :].unsqueeze(1).to_broadcast(shape),
                    op=ALU.mult,
                )
                nc.vector.tensor_tensor(
                    out=rot[:, tile_range, qk, OTHER, :].rearrange("p n (t i) -> p n t i", t=2),
                    in0=sin_sb[:, tile_range, :].rearrange("p n (i t) -> p n t i", t=2),
                    in1=gain_other[:, m, :, :].unsqueeze(1).to_broadcast(shape),
                    op=ALU.mult,
                )

        act_words = act_sb[:].bitcast(F32)
        act_codes = keep.tile([P, PASSES, TOKEN_TILES * P], U32, align_bytes=64)
        act_scales = keep.tile([P, PASSES, TOKEN_TILES * P], U8, align_bytes=64)

        def quantise_activations(first_tile):
            grouped = stage.tile([P, PASSES, 2 * P, PACK], BF16, name="act_grouped", align_bytes=64)
            grouped_words = grouped[:].bitcast(F32)
            for j in range(2):
                turned = psum_t.tile([P, PASSES * 2, P], F32, name="turned")
                for w in range(PASSES * 2):
                    nc.tensor.transpose(
                        out=turned[:, w, :],
                        in_=act_words[:, first_tile + j, w * P : (w + 1) * P],
                        identity=ident[:],
                    )
                nc.scalar.copy(
                    out=grouped_words[:, :, j * P : (j + 1) * P, :],
                    in_=turned[:].rearrange("p (g u) r -> p g r u", u=2),
                )
            cols = slice(first_tile * P, (first_tile + 2) * P)
            for g in range(PASSES):
                nc.vector.quantize_mx(
                    out=act_codes[:, g, cols].bitcast(FP8X4),
                    scales=act_scales[:, g, cols],
                    in_=grouped[:, g, :, :].rearrange("p r j -> p (r j)"),
                )

        w_codes = keep.tile([P, 4, PASSES, HD], U32, align_bytes=64)
        w_scales = keep.tile([P, 4, PASSES, HD], U8, align_bytes=64)

        def quantise_weight_pass(raw, m, g):
            grouped = stage.tile([P, HD, PACK], BF16, name="w_grouped", align_bytes=64)
            dst = grouped[:].rearrange("p (c i) t -> p c t i", i=4)
            src = raw[:, g, :, :].rearrange("p t (c i) -> p c t i", i=4)
            split = VECTOR_COLS // 4
            nc.vector.tensor_copy(out=dst[:, :split], in_=src[:, :split])
            nc.scalar.copy(out=dst[:, split:], in_=src[:, split:])
            for bank in range(HD // BANK):
                cols = slice(bank * BANK, (bank + 1) * BANK)
                nc.vector.quantize_mx(
                    out=w_codes[:, m, g, cols].bitcast(FP8X4),
                    scales=w_scales[:, m, g, cols],
                    in_=grouped[:, cols, :].rearrange("p c t -> p (c t)"),
                )

        units = [(TEXT_TILES + j, 0, qk) for qk in range(2) for j in range(IMAGE_TILES)]
        units += [(n, 1, qk) for qk in range(2) for n in range(TEXT_TILES)]
        in_psum = {}
        in_sbuf = {}

        def multiply(u):
            n, stream, qk = units[u]
            m = 2 * stream + qk
            rot_ps = psum_rot.tile([P, 2, D], F32, name="rot_ps")
            nc.tensor.matmul(
                out=rot_ps[:].rearrange("p s d -> p (s d)"),
                lhsT=ident[:],
                rhs=rot[:, n, qk, :, :].rearrange("p s d -> p (s d)"),
                start=True,
                stop=True,
            )
            tokens = slice(n * P, (n + 1) * P)
            banks = []
            for bank in range(HD // BANK):
                cols = slice(bank * BANK, (bank + 1) * BANK)
                acc = psum_y.tile([P, BANK], F32, name="acc")
                for g in range(PASSES):
                    nc.tensor.matmul_mx(
                        out=acc[:],
                        lhsT=act_codes[:, g, tokens].bitcast(FP8X4),
                        lhsT_scale=act_scales[:, g, tokens],
                        rhs=w_codes[:, m, g, cols].bitcast(FP8X4),
                        rhs_scale=w_scales[:, m, g, cols],
                        start=(g == 0),
                        stop=(g == PASSES - 1),
                    )
                banks.append(acc)
            in_psum[u] = (rot_ps, banks)

        def bias_squares_products(u):
            n, stream, qk = units[u]
            m = 2 * stream + qk
            rot_ps, banks = in_psum[u]
            y = work.tile([P, H, 2, PAIRS], F32, name="y")
            for bank in range(HD // BANK):
                heads = slice(bank * BANK_HEADS, (bank + 1) * BANK_HEADS)
                nc.vector.tensor_tensor(
                    out=y[:, heads, :, :],
                    in0=banks[bank][:].rearrange("p (h i t) -> p h t i", h=BANK_HEADS, t=2),
                    in1=bias_bc[:, m, heads, :, :],
                    op=ALU.add,
                )
            sumsq = work.tile([P, H], F32, name="sumsq", bufs=4)
            for h in range(H):
                squares = work.tile([P, D], BF16, name="squares")
                nc.scalar.activation(
                    out=squares[:],
                    in_=y[:, h, :, :].rearrange("p t i -> p (t i)"),
                    func=ACT.Square,
                    accum_out=sumsq[:, h : h + 1],
                )
            inv_rms = work.tile([P, H], F32, name="inv_rms", bufs=4)
            nc.scalar.activation(
                out=inv_rms[:], in_=sumsq[:], func=ACT.Abs_reciprocal_sqrt, bias=eps_col[:, 0:1], scale=1.0 / D
            )
            same = work.tile([P, H, 2, PAIRS], F32, name="same", bufs=4)
            nc.vector.tensor_tensor(
                out=same[:].rearrange("p h t i -> p h (t i)"),
                in0=y[:].rearrange("p h t i -> p h (t i)"),
                in1=rot_ps[:, SAME, :].unsqueeze(1).to_broadcast([P, H, D]),
                op=ALU.mult,
            )
            other = work.tile([P, H, 2, PAIRS], F32, name="other")
            nc.vector.tensor_tensor(
                out=other[:, :, 0, :],
                in0=y[:, :, 1, :],
                in1=rot_ps[:, OTHER, :PAIRS].unsqueeze(1).to_broadcast([P, H, PAIRS]),
                op=ALU.mult,
            )
            if stream == 0:
                nc.gpsimd.tensor_tensor(
                    out=other[:, :, 1, :],
                    in0=y[:, :, 0, :],
                    in1=rot[:, n, qk, OTHER, PAIRS:].unsqueeze(1).to_broadcast([P, H, PAIRS]),
                    op=ALU.mult,
                )
            else:
                nc.vector.tensor_tensor(
                    out=other[:, :, 1, :],
                    in0=y[:, :, 0, :],
                    in1=rot_ps[:, OTHER, PAIRS:].unsqueeze(1).to_broadcast([P, H, PAIRS]),
                    op=ALU.mult,
                )
            in_sbuf[u] = (same, other, inv_rms)

        def add_products(u):
            same, other, inv_rms = in_sbuf[u]
            nc.gpsimd.tensor_tensor(out=same[:], in0=same[:], in1=other[:], op=ALU.add)

        def normalise_store(u):
            n, stream, qk = units[u]
            same, other, inv_rms = in_sbuf[u]
            result = work.tile([P, H, PAIRS, 2], F32, name="result")
            for h in range(H):
                nc.scalar.activation(
                    out=result[:, h, :, :],
                    in_=same[:, h, :, :].rearrange("p t i -> p i t"),
                    func=ACT.Copy,
                    scale=inv_rms[:, h : h + 1],
                )
            tile_lo, tiles = STREAM_TILES[stream]
            out_rows = token_rows(outs[qk].rearrange("b s h d -> (b s) (h d)"), tile_lo, tiles)
            nc.scalar.dma_start(out=out_rows[:, n - tile_lo, :], in_=result[:].rearrange("p h i t -> p (h i t)"))

        build_tables(0)
        quantise_activations(TEXT_TILES)
        for g in range(PASSES):
            quantise_weight_pass(raw_q, 0, g)
        spread_bias(0)
        raws = {1: raw_k, 2: load_weight(2)}

        multiply(0)
        for s in range(len(units) + 2):
            if s + 1 < len(units):
                multiply(s + 1)
            if 1 <= s <= len(units):
                add_products(s - 1)
            if s >= 2:
                normalise_store(s - 2)
            if s < len(units):
                bias_squares_products(s)
            if s == 0:
                quantise_activations(TEXT_TILES + 2)
                quantise_activations(TEXT_TILES + 4)
            elif s <= 2:
                quantise_weight_pass(raws[1], 1, s - 1)
            elif s == 3:
                raws[3] = load_weight(3)
                spread_bias(1)
                quantise_activations(0)
            elif s <= 5:
                quantise_weight_pass(raws[2], 2, s - 4)
            elif s == 6:
                build_tables(1)
                spread_bias(2)
                spread_bias(3)
            elif s <= 8:
                quantise_weight_pass(raws[3], 3, s - 7)
